import numpy as np
import ml_dtypes


def mxq(x, axis, fmt="e4m3"):
    dtype, down = {"e4m3": (ml_dtypes.float8_e4m3fn, 7), "e5m2": (ml_dtypes.float8_e5m2, 14)}[fmt]
    v = np.moveaxis(np.asarray(x, np.float32).astype(ml_dtypes.bfloat16).astype(np.float64), axis, -1)
    blocks = v.reshape(v.shape[:-1] + (-1, 32))
    amax = np.abs(blocks).max(-1, keepdims=True)
    byte = np.maximum(np.where(amax > 0, np.frexp(amax)[1] - 1 + 127, 0) - down, 1)
    scale = np.exp2(byte - 127.0)
    codes = (blocks / scale).astype(np.float32).astype(dtype).astype(np.float64)
    return np.moveaxis((codes * scale).reshape(v.shape), -1, axis)


WIDE = False


def mx_kscale(k):
    if not WIDE:
        return np.ones(k)
    levels = np.array([10, -10, 5, -5, 0])
    if k % 512:
        return np.exp2(np.random.permutation(np.resize(levels, k // 32))).repeat(32)
    a = np.empty((k // 512, 16))
    for p in range(k // 512):
        a[p, :8] = np.random.permutation(np.resize(levels, 8))
        for g in range(8):
            far = levels[np.abs(levels - a[p, g]) >= 10]
            a[p, g + 8] = far[np.random.randint(len(far))]
    return np.exp2(a.ravel()).repeat(32)


BF16 = ml_dtypes.bfloat16


def bf(x):
    return np.asarray(x, np.float32).astype(BF16)


def f64(x):
    return np.asarray(x).astype(np.float64)


N, K, C, CE, M, F = 128, 32, 512, 1536, 512, 2048
SCALE = 30.0
EPS = 1e-5


def erf(x):
    a = np.minimum(np.abs(x), 6.0)
    a2 = 2.0 * a * a
    t = a
    s = a
    for n in range(1, 110):
        t = t * a2 / (2 * n + 1)
        s = s + t
    return np.sign(x) * np.minimum(s * np.exp(-a * a) * 2.0 / np.sqrt(np.pi), 1.0)


def gelu(v):
    return 0.5 * v * (1.0 + erf(v / np.sqrt(2.0)))


def layernorm(x, w, b):
    mu = x.mean(-1, keepdims=True)
    var = ((x - mu) ** 2).mean(-1, keepdims=True)
    return (x - mu) / np.sqrt(var + EPS) * w + b


def setup_inputs():
    s = mx_kscale(M)
    return {
        "m2": bf(gelu(np.random.standard_normal((N, K, M))) * s),
        "W3": bf(np.random.standard_normal((C, M)) * 3.0 / np.sqrt(M) / s),
        "b3": bf(np.random.standard_normal(C) * 0.1),
        "attention_mask": bf(np.random.random((N, K)) < 0.75),
        "node_features": bf(np.random.standard_normal((N, C))),
        "ln1_w": bf(1.0 + np.random.standard_normal(C) * 0.1),
        "ln1_b": bf(np.random.standard_normal(C) * 0.1),
    }


def reference(m2, W3, b3, attention_mask, node_features, ln1_w, ln1_b):
    m = (mxq(f64(m2), 2, "e4m3") @ mxq(f64(W3).T, 0, "e4m3")) + f64(b3)
    m = f64(attention_mask)[..., None] * m
    agg = m.sum(-2) / SCALE
    return layernorm(f64(node_features) + agg, f64(ln1_w), f64(ln1_b))

@@ -1,0 +1,181 @@
+from contextlib import ExitStack
+
+import concourse.mybir as mybir
+from concourse.masks import make_identity
+
+F32 = mybir.dt.float32
+BF16 = mybir.dt.bfloat16
+U32 = mybir.dt.uint32
+U8 = mybir.dt.uint8
+FP8X4 = mybir.dt.float8_e4m3fn_x4
+ALU = mybir.AluOpType
+ACT = mybir.ActivationFunctionType
+
+P = 128
+NEIGHBOURS = 32
+K = 512
+CHANNELS = 512
+PACK = 4
+WORDS = K // 2
+HALVES = WORDS // P
+UNIT_SLABS = 2
+UNITS = NEIGHBOURS // UNIT_SLABS
+W3_UNITS = CHANNELS // (P * UNIT_SLABS)
+RUN = 4
+LAG = 2
+SCALE = 30.0
+EPS = 1e-5
+
+FLOPS = 2 * P * NEIGHBOURS * K * CHANNELS
+
+
+def tile_decoderlayer_pb_kernel(
+    tc, m2, W3, b3, attention_mask, node_features, ln1_w, ln1_b, out
+):
+    nc = tc.nc
+    with ExitStack() as ctx:
+        ctx.enter_context(tc.manual_schedule())
+        keep = ctx.enter_context(tc.tile_pool(name="keep", bufs=1))
+        grouped_pool = ctx.enter_context(tc.tile_pool(name="grouped", bufs=4))
+        mx_pool = ctx.enter_context(tc.tile_pool(name="mx", bufs=UNITS))
+        bank_pool = ctx.enter_context(tc.psum_pool(name="banks", bufs=7))
+        acc_pool = ctx.enter_context(tc.psum_pool(name="acc", bufs=1))
+
+        mask_bf = keep.tile([P, NEIGHBOURS], BF16)
+        nc.sync.dma_start(out=mask_bf[:], in_=attention_mask)
+        w3_rows = []
+        for w in range(W3_UNITS):
+            rows = keep.tile([P, UNIT_SLABS * K], BF16, name="w3_rows%d" % w)
+            nc.sync.dma_start(
+                out=rows[:].rearrange("p (s k) -> p s k", s=UNIT_SLABS),
+                in_=W3[w * UNIT_SLABS * P : (w + 1) * UNIT_SLABS * P, :].rearrange(
+                    "(s p) k -> p s k", p=P
+                ),
+            )
+            w3_rows.append(rows)
+        m2_rows = []
+        for i in range(UNITS):
+            rows = keep.tile([P, UNIT_SLABS * K], BF16, name="m2_rows%d" % i)
+            nc.sync.dma_start(
+                out=rows[:].rearrange("p (s k) -> p s k", s=UNIT_SLABS),
+                in_=m2[:, i * UNIT_SLABS : (i + 1) * UNIT_SLABS, :],
+            )
+            m2_rows.append(rows)
+        nodes_bf = keep.tile([P, CHANNELS], BF16)
+        nc.sync.dma_start(out=nodes_bf[:], in_=node_features)
+        b3_all = keep.tile([P, CHANNELS], BF16)
+        nc.sync.dma_start(out=b3_all[:], in_=b3.partition_broadcast(P))
+        gain_all = keep.tile([P, CHANNELS], BF16)
+        nc.sync.dma_start(out=gain_all[:], in_=ln1_w.partition_broadcast(P))
+        shift_all = keep.tile([P, CHANNELS], BF16)
+        nc.sync.dma_start(out=shift_all[:], in_=ln1_b.partition_broadcast(P))
+
+        identity = keep.tile([P, P], F32)
+        make_identity(nc, identity[:])
+        eps = keep.tile([P, 1], F32)
+        nc.vector.memset(eps[:], EPS)
+        table_warm = keep.tile([P, 1], F32)
+        nc.scalar.sqrt(out=table_warm[:], in_=eps[:])
+        mask = keep.tile([P, NEIGHBOURS], F32)
+        nc.vector.tensor_copy(out=mask[:], in_=mask_bf[:])
+        kept_nodes = keep.tile([P, NEIGHBOURS, P], F32)
+        for k in range(NEIGHBOURS):
+            nc.vector.tensor_scalar_mul(
+                out=kept_nodes[:, k, :], in0=identity[:], scalar1=mask[:, k : k + 1]
+            )
+
+        def transpose_unit(rows, selections):
+            words = rows[:].bitcast(F32)
+            bank = bank_pool.tile([P, UNIT_SLABS, HALVES, P], F32)
+            for s in range(UNIT_SLABS):
+                for u in range(HALVES):
+                    block = slice(s * WORDS + u, (s + 1) * WORDS, HALVES)
+                    nc.tensor.transpose(bank[:, s, u, :], words[:, block], selections[s])
+            return bank
+
+        def regroup_unit(bank):
+            grouped = grouped_pool.tile([P, UNIT_SLABS * P * PACK], BF16, align_bytes=64)
+            nc.scalar.copy(
+                out=grouped[:].bitcast(F32).rearrange("p (s r u) -> p s r u", s=UNIT_SLABS, u=HALVES),
+                in_=bank[:].rearrange("p s u r -> p s r u"),
+            )
+            return grouped
+
+        def quantise_unit(grouped, codes, scales):
+            nc.vector.quantize_mx(out=codes.bitcast(FP8X4), scales=scales, in_=grouped[:])
+
+        w3_codes = keep.tile([P, CHANNELS], U32, align_bytes=64)
+        w3_scales = keep.tile([P, CHANNELS], U8, align_bytes=64)
+        for w in range(W3_UNITS):
+            channels = slice(w * UNIT_SLABS * P, (w + 1) * UNIT_SLABS * P)
+            bank = transpose_unit(w3_rows[w], [identity[:]] * UNIT_SLABS)
+            quantise_unit(regroup_unit(bank), w3_codes[:, channels], w3_scales[:, channels])
+
+        acc = acc_pool.tile([P, CHANNELS], F32)
+        m2_codes = {}
+        m2_scales = {}
+
+        def prepare_unit(i):
+            selections = [kept_nodes[:, i * UNIT_SLABS + s, :] for s in range(UNIT_SLABS)]
+            bank = transpose_unit(m2_rows[i], selections)
+            codes = mx_pool.tile([P, UNIT_SLABS * P], U32, align_bytes=64)
+            scales = mx_pool.tile([P, UNIT_SLABS * P], U8, align_bytes=64)
+            quantise_unit(regroup_unit(bank), codes[:], scales[:])
+            m2_codes[i] = codes
+            m2_scales[i] = scales
+
+        def multiply_unit(i):
+            for s in range(UNIT_SLABS):
+                neighbour = i * UNIT_SLABS + s
+                nodes = slice(s * P, (s + 1) * P)
+                nc.tensor.matmul_mx(
+                    out=acc[:],
+                    lhsT=m2_codes[i][:, nodes].bitcast(FP8X4),
+                    lhsT_scale=m2_scales[i][:, nodes],
+                    rhs=w3_codes[:].bitcast(FP8X4),
+                    rhs_scale=w3_scales[:],
+                    start=(neighbour == 0),
+                    stop=(neighbour == NEIGHBOURS - 1),
+                )
+
+        multiplied = 0
+        for first in range(0, UNITS, RUN):
+            for i in range(first, first + RUN):
+                prepare_unit(i)
+            ready = UNITS if first + RUN == UNITS else first + RUN - LAG
+            for i in range(multiplied, ready):
+                multiply_unit(i)
+            multiplied = ready
+
+        kept = keep.tile([P, 1], F32)
+        nc.vector.tensor_reduce(out=kept[:], in_=mask[:], axis=mybir.AxisListType.X, op=ALU.add)
+        kept_scaled = keep.tile([P, 1], F32)
+        nc.vector.tensor_scalar_mul(out=kept_scaled[:], in0=kept[:], scalar1=1.0 / SCALE)
+        base = keep.tile([P, CHANNELS], F32)
+        nc.vector.scalar_tensor_tensor(
+            out=base[:], in0=b3_all[:], scalar=kept_scaled[:], in1=nodes_bf[:], op0=ALU.mult, op1=ALU.add
+        )
+
+        x = keep.tile([P, CHANNELS], F32)
+        nc.vector.scalar_tensor_tensor(
+            out=x[:], in0=acc[:], scalar=1.0 / SCALE, in1=base[:], op0=ALU.mult, op1=ALU.add
+        )
+        stats = keep.tile([P, 6], F32)
+        nc.vector.bn_stats(out=stats[:], in_=x[:])
+        mean_var = keep.tile([P, 2], F32)
+        nc.vector.bn_aggr(out=mean_var[:], in_=stats[:])
+        std = keep.tile([P, 1], F32)
+        nc.scalar.activation(out=std[:], in_=mean_var[:, 1:2], func=ACT.Sqrt, bias=eps[:], scale=1.0)
+        centred = keep.tile([P, CHANNELS], F32)
+        nc.vector.scalar_tensor_tensor(
+            out=centred[:], in0=x[:], scalar=mean_var[:, 0:1], in1=gain_all[:],
+            op0=ALU.subtract, op1=ALU.mult,
+        )
+        inv_std = keep.tile([P, 1], F32)
+        nc.vector.reciprocal(out=inv_std[:], in_=std[:])
+        result = keep.tile([P, CHANNELS], F32)
+        nc.vector.scalar_tensor_tensor(
+            out=result[:], in0=centred[:], scalar=inv_std[:], in1=shift_all[:],
+            op0=ALU.mult, op1=ALU.add,
+        )
+        nc.sync.dma_start(out=out, in_=result[:])

@@ -18,10 +18,12 @@ CHANNELS = 512
 PACK = 4
 WORDS = K // 2
 HALVES = WORDS // P
+GROUPS = K // 32
 UNIT_SLABS = 2
 UNITS = NEIGHBOURS // UNIT_SLABS
 W3_UNITS = CHANNELS // (P * UNIT_SLABS)
 RUN = 4
+AHEAD = 3
 LAG = 2
 SCALE = 30.0
 EPS = 1e-5
@@ -37,6 +39,7 @@ def tile_decoderlayer_pb_kernel(
         ctx.enter_context(tc.manual_schedule())
         keep = ctx.enter_context(tc.tile_pool(name="keep", bufs=1))
         grouped_pool = ctx.enter_context(tc.tile_pool(name="grouped", bufs=4))
+        split_pool = ctx.enter_context(tc.tile_pool(name="split", bufs=AHEAD + 4))
         mx_pool = ctx.enter_context(tc.tile_pool(name="mx", bufs=UNITS))
         bank_pool = ctx.enter_context(tc.psum_pool(name="banks", bufs=7))
         acc_pool = ctx.enter_context(tc.psum_pool(name="acc", bufs=1))
@@ -78,19 +81,26 @@ def tile_decoderlayer_pb_kernel(
         nc.scalar.sqrt(out=table_warm[:], in_=eps[:])
         mask = keep.tile([P, NEIGHBOURS], F32)
         nc.vector.tensor_copy(out=mask[:], in_=mask_bf[:])
-        kept_nodes = keep.tile([P, NEIGHBOURS, P], F32)
-        for k in range(NEIGHBOURS):
-            nc.vector.tensor_scalar_mul(
-                out=kept_nodes[:, k, :], in0=identity[:], scalar1=mask[:, k : k + 1]
-            )
 
-        def transpose_unit(rows, selections):
-            words = rows[:].bitcast(F32)
+        def split_unit(rows, row_factors):
+            split = split_pool.tile([P, UNIT_SLABS * K], BF16)
+            for s in range(UNIT_SLABS):
+                values = slice(s * K, (s + 1) * K)
+                source = rows[:, values].rearrange("p (g u e) -> p u g e", g=GROUPS, u=HALVES)
+                target = split[:, values].rearrange("p (u g e) -> p u g e", u=HALVES, g=GROUPS)
+                if row_factors is None:
+                    nc.vector.tensor_copy(out=target, in_=source)
+                else:
+                    nc.vector.tensor_scalar_mul(out=target, in0=source, scalar1=row_factors[s])
+            return split
+
+        def transpose_unit(split):
+            words = split[:].bitcast(F32)
             bank = bank_pool.tile([P, UNIT_SLABS, HALVES, P], F32)
             for s in range(UNIT_SLABS):
                 for u in range(HALVES):
-                    block = slice(s * WORDS + u, (s + 1) * WORDS, HALVES)
-                    nc.tensor.transpose(bank[:, s, u, :], words[:, block], selections[s])
+                    block = slice(s * WORDS + u * P, s * WORDS + (u + 1) * P)
+                    nc.tensor.transpose(bank[:, s, u, :], words[:, block], identity[:])
             return bank
 
         def regroup_unit(bank):
@@ -106,18 +116,24 @@ def tile_decoderlayer_pb_kernel(
 
         w3_codes = keep.tile([P, CHANNELS], U32, align_bytes=64)
         w3_scales = keep.tile([P, CHANNELS], U8, align_bytes=64)
+        w3_split = [split_unit(w3_rows[w], None) for w in range(W3_UNITS)]
         for w in range(W3_UNITS):
             channels = slice(w * UNIT_SLABS * P, (w + 1) * UNIT_SLABS * P)
-            bank = transpose_unit(w3_rows[w], [identity[:]] * UNIT_SLABS)
+            bank = transpose_unit(w3_split[w])
             quantise_unit(regroup_unit(bank), w3_codes[:, channels], w3_scales[:, channels])
 
         acc = acc_pool.tile([P, CHANNELS], F32)
         m2_codes = {}
         m2_scales = {}
+        m2_split = {}
+
+        def split_m2_unit(i):
+            first = i * UNIT_SLABS
+            row_factors = [mask[:, first + s : first + s + 1] for s in range(UNIT_SLABS)]
+            m2_split[i] = split_unit(m2_rows[i], row_factors)
 
         def prepare_unit(i):
-            selections = [kept_nodes[:, i * UNIT_SLABS + s, :] for s in range(UNIT_SLABS)]
-            bank = transpose_unit(m2_rows[i], selections)
+            bank = transpose_unit(m2_split[i])
             codes = mx_pool.tile([P, UNIT_SLABS * P], U32, align_bytes=64)
             scales = mx_pool.tile([P, UNIT_SLABS * P], U8, align_bytes=64)
             quantise_unit(regroup_unit(bank), codes[:], scales[:])
@@ -139,8 +155,12 @@ def tile_decoderlayer_pb_kernel(
                 )
 
         multiplied = 0
+        for i in range(AHEAD):
+            split_m2_unit(i)
         for first in range(0, UNITS, RUN):
             for i in range(first, first + RUN):
+                if i + AHEAD < UNITS:
+                    split_m2_unit(i + AHEAD)
                 prepare_unit(i)
             ready = UNITS if first + RUN == UNITS else first + RUN - LAG
             for i in range(multiplied, ready):

@@ -15,6 +15,7 @@ P = 128
 NEIGHBOURS = 32
 K = 512
 CHANNELS = 512
+HALF = CHANNELS // 2
 PACK = 4
 WORDS = K // 2
 HALVES = WORDS // P
@@ -25,6 +26,7 @@ W3_UNITS = CHANNELS // (P * UNIT_SLABS)
 RUN = 4
 AHEAD = 3
 LAG = 2
+TAIL = 3
 SCALE = 30.0
 EPS = 1e-5
 
@@ -41,7 +43,7 @@ def tile_decoderlayer_pb_kernel(
         grouped_pool = ctx.enter_context(tc.tile_pool(name="grouped", bufs=4))
         split_pool = ctx.enter_context(tc.tile_pool(name="split", bufs=AHEAD + 4))
         mx_pool = ctx.enter_context(tc.tile_pool(name="mx", bufs=UNITS))
-        bank_pool = ctx.enter_context(tc.psum_pool(name="banks", bufs=7))
+        bank_pool = ctx.enter_context(tc.psum_pool(name="banks", bufs=5))
         acc_pool = ctx.enter_context(tc.psum_pool(name="acc", bufs=1))
 
         mask_bf = keep.tile([P, NEIGHBOURS], BF16)
@@ -78,7 +80,9 @@ def tile_decoderlayer_pb_kernel(
         eps = keep.tile([P, 1], F32)
         nc.vector.memset(eps[:], EPS)
         table_warm = keep.tile([P, 1], F32)
-        nc.scalar.sqrt(out=table_warm[:], in_=eps[:])
+        nc.scalar.activation(
+            out=table_warm[:], in_=eps[:], func=ACT.Abs_reciprocal_sqrt, bias=eps[:], scale=1.0
+        )
         mask = keep.tile([P, NEIGHBOURS], F32)
         nc.vector.tensor_copy(out=mask[:], in_=mask_bf[:])
 
@@ -117,12 +121,14 @@ def tile_decoderlayer_pb_kernel(
         w3_codes = keep.tile([P, CHANNELS], U32, align_bytes=64)
         w3_scales = keep.tile([P, CHANNELS], U8, align_bytes=64)
         w3_split = [split_unit(w3_rows[w], None) for w in range(W3_UNITS)]
-        for w in range(W3_UNITS):
+        w3_grouped = [regroup_unit(transpose_unit(w3_split[w])) for w in range(W3_UNITS)]
+
+        def quantise_w3_unit(w):
             channels = slice(w * UNIT_SLABS * P, (w + 1) * UNIT_SLABS * P)
-            bank = transpose_unit(w3_split[w])
-            quantise_unit(regroup_unit(bank), w3_codes[:, channels], w3_scales[:, channels])
+            quantise_unit(w3_grouped[w], w3_codes[:, channels], w3_scales[:, channels])
 
         acc = acc_pool.tile([P, CHANNELS], F32)
+        acc_tail = [acc_pool.tile([P, HALF], F32, name="acc_tail%d" % h) for h in range(2)]
         m2_codes = {}
         m2_scales = {}
         m2_split = {}
@@ -140,62 +146,79 @@ def tile_decoderlayer_pb_kernel(
             m2_codes[i] = codes
             m2_scales[i] = scales
 
-        def multiply_unit(i):
+        def multiply_unit(i, group, channels, first_unit, last_unit):
             for s in range(UNIT_SLABS):
-                neighbour = i * UNIT_SLABS + s
                 nodes = slice(s * P, (s + 1) * P)
                 nc.tensor.matmul_mx(
-                    out=acc[:],
+                    out=group[:],
                     lhsT=m2_codes[i][:, nodes].bitcast(FP8X4),
                     lhsT_scale=m2_scales[i][:, nodes],
-                    rhs=w3_codes[:].bitcast(FP8X4),
-                    rhs_scale=w3_scales[:],
-                    start=(neighbour == 0),
-                    stop=(neighbour == NEIGHBOURS - 1),
+                    rhs=w3_codes[:, channels].bitcast(FP8X4),
+                    rhs_scale=w3_scales[:, channels],
+                    start=(i == first_unit and s == 0),
+                    stop=(i == last_unit and s == UNIT_SLABS - 1),
                 )
 
+        base = keep.tile([P, CHANNELS], F32)
+
+        def residual():
+            kept = keep.tile([P, 1], F32)
+            nc.vector.tensor_reduce(out=kept[:], in_=mask[:], axis=mybir.AxisListType.X, op=ALU.add)
+            kept_scaled = keep.tile([P, 1], F32)
+            nc.vector.tensor_scalar_mul(out=kept_scaled[:], in0=kept[:], scalar1=1.0 / SCALE)
+            nc.vector.scalar_tensor_tensor(
+                out=base[:], in0=b3_all[:], scalar=kept_scaled[:], in1=nodes_bf[:], op0=ALU.mult, op1=ALU.add
+            )
+
+        main_units = UNITS - TAIL
         multiplied = 0
         for i in range(AHEAD):
             split_m2_unit(i)
+            if i < W3_UNITS:
+                quantise_w3_unit(i)
         for first in range(0, UNITS, RUN):
             for i in range(first, first + RUN):
                 if i + AHEAD < UNITS:
                     split_m2_unit(i + AHEAD)
+                    if i + AHEAD == UNITS - 1:
+                        residual()
                 prepare_unit(i)
-            ready = UNITS if first + RUN == UNITS else first + RUN - LAG
+            ready = main_units if first + RUN == UNITS else first + RUN - LAG
             for i in range(multiplied, ready):
-                multiply_unit(i)
+                multiply_unit(i, acc, slice(0, CHANNELS), 0, main_units - 1)
             multiplied = ready
+        halves = [slice(h * HALF, (h + 1) * HALF) for h in range(2)]
+        for h in range(2):
+            for i in range(main_units, UNITS):
+                multiply_unit(i, acc_tail[h], halves[h], main_units, UNITS - 1)
 
-        kept = keep.tile([P, 1], F32)
-        nc.vector.tensor_reduce(out=kept[:], in_=mask[:], axis=mybir.AxisListType.X, op=ALU.add)
-        kept_scaled = keep.tile([P, 1], F32)
-        nc.vector.tensor_scalar_mul(out=kept_scaled[:], in0=kept[:], scalar1=1.0 / SCALE)
-        base = keep.tile([P, CHANNELS], F32)
+        x_main = keep.tile([P, CHANNELS], F32)
         nc.vector.scalar_tensor_tensor(
-            out=base[:], in0=b3_all[:], scalar=kept_scaled[:], in1=nodes_bf[:], op0=ALU.mult, op1=ALU.add
+            out=x_main[:], in0=acc[:], scalar=1.0 / SCALE, in1=base[:], op0=ALU.mult, op1=ALU.add
         )
-
         x = keep.tile([P, CHANNELS], F32)
-        nc.vector.scalar_tensor_tensor(
-            out=x[:], in0=acc[:], scalar=1.0 / SCALE, in1=base[:], op0=ALU.mult, op1=ALU.add
-        )
-        stats = keep.tile([P, 6], F32)
-        nc.vector.bn_stats(out=stats[:], in_=x[:])
+        stats = keep.tile([P, 2, 6], F32)
+        for h in range(2):
+            nc.vector.scalar_tensor_tensor(
+                out=x[:, halves[h]], in0=acc_tail[h][:], scalar=1.0 / SCALE, in1=x_main[:, halves[h]],
+                op0=ALU.mult, op1=ALU.add,
+            )
+            nc.vector.bn_stats(out=stats[:, h, :], in_=x[:, halves[h]])
         mean_var = keep.tile([P, 2], F32)
-        nc.vector.bn_aggr(out=mean_var[:], in_=stats[:])
-        std = keep.tile([P, 1], F32)
-        nc.scalar.activation(out=std[:], in_=mean_var[:, 1:2], func=ACT.Sqrt, bias=eps[:], scale=1.0)
+        nc.vector.bn_aggr(out=mean_var[:], in_=stats[:].rearrange("p h s -> p (h s)"))
+        inv_std = keep.tile([P, 1], F32)
+        nc.scalar.activation(
+            out=inv_std[:], in_=mean_var[:, 1:2], func=ACT.Abs_reciprocal_sqrt, bias=eps[:], scale=1.0
+        )
         centred = keep.tile([P, CHANNELS], F32)
         nc.vector.scalar_tensor_tensor(
             out=centred[:], in0=x[:], scalar=mean_var[:, 0:1], in1=gain_all[:],
             op0=ALU.subtract, op1=ALU.mult,
         )
-        inv_std = keep.tile([P, 1], F32)
-        nc.vector.reciprocal(out=inv_std[:], in_=std[:])
         result = keep.tile([P, CHANNELS], F32)
-        nc.vector.scalar_tensor_tensor(
-            out=result[:], in0=centred[:], scalar=inv_std[:], in1=shift_all[:],
-            op0=ALU.mult, op1=ALU.add,
-        )
-        nc.sync.dma_start(out=out, in_=result[:])
+        for channels, queue in zip(halves, (nc.sync, nc.scalar)):
+            nc.vector.scalar_tensor_tensor(
+                out=result[:, channels], in0=centred[:, channels], scalar=inv_std[:],
+                in1=shift_all[:, channels], op0=ALU.mult, op1=ALU.add,
+            )
+            queue.dma_start(out=out[:, channels], in_=result[:, channels])

@@ -27,6 +27,7 @@ RUN = 4
 AHEAD = 3
 LAG = 2
 TAIL = 3
+WARM_FIRST = 5
 SCALE = 30.0
 EPS = 1e-5
 
@@ -75,6 +76,8 @@ def tile_decoderlayer_pb_kernel(
         shift_all = keep.tile([P, CHANNELS], BF16)
         nc.sync.dma_start(out=shift_all[:], in_=ln1_b.partition_broadcast(P))
 
+        zeros = keep.tile([P, CHANNELS], BF16)
+        nc.vector.memset(zeros[:], 0.0)
         identity = keep.tile([P, P], F32)
         make_identity(nc, identity[:])
         eps = keep.tile([P, 1], F32)
@@ -118,6 +121,15 @@ def tile_decoderlayer_pb_kernel(
         def quantise_unit(grouped, codes, scales):
             nc.vector.quantize_mx(out=codes.bitcast(FP8X4), scales=scales, in_=grouped[:])
 
+        acc = acc_pool.tile([P, CHANNELS], F32)
+        acc_tail = [acc_pool.tile([P, HALF], F32, name="acc_tail%d" % h) for h in range(2)]
+
+        def keep_clock(matmuls):
+            for j in range(matmuls):
+                nc.tensor.matmul(out=acc[:], lhsT=zeros[:, :P], rhs=zeros[:], start=True, stop=True)
+
+        keep_clock(WARM_FIRST)
+
         w3_codes = keep.tile([P, CHANNELS], U32, align_bytes=64)
         w3_scales = keep.tile([P, CHANNELS], U8, align_bytes=64)
         w3_split = [split_unit(w3_rows[w], None) for w in range(W3_UNITS)]
@@ -127,8 +139,6 @@ def tile_decoderlayer_pb_kernel(
             channels = slice(w * UNIT_SLABS * P, (w + 1) * UNIT_SLABS * P)
             quantise_unit(w3_grouped[w], w3_codes[:, channels], w3_scales[:, channels])
 
-        acc = acc_pool.tile([P, CHANNELS], F32)
-        acc_tail = [acc_pool.tile([P, HALF], F32, name="acc_tail%d" % h) for h in range(2)]
         m2_codes = {}
         m2_scales = {}
         m2_split = {}
@@ -183,6 +193,8 @@ def tile_decoderlayer_pb_kernel(
                     if i + AHEAD == UNITS - 1:
                         residual()
                 prepare_unit(i)
+                if first == 0 and i + 1 < RUN:
+                    keep_clock(1)
             ready = main_units if first + RUN == UNITS else first + RUN - LAG
             for i in range(multiplied, ready):
                 multiply_unit(i, acc, slice(0, CHANNELS), 0, main_units - 1)

@@ -27,7 +27,8 @@ RUN = 4
 AHEAD = 3
 LAG = 2
 TAIL = 3
-WARM_FIRST = 5
+WARM_FIRST = 8
+WARM_NEXT = 2
 SCALE = 30.0
 EPS = 1e-5
 
@@ -47,18 +48,18 @@ def tile_decoderlayer_pb_kernel(
         bank_pool = ctx.enter_context(tc.psum_pool(name="banks", bufs=5))
         acc_pool = ctx.enter_context(tc.psum_pool(name="acc", bufs=1))
 
-        mask_bf = keep.tile([P, NEIGHBOURS], BF16)
-        nc.sync.dma_start(out=mask_bf[:], in_=attention_mask)
         w3_rows = []
         for w in range(W3_UNITS):
             rows = keep.tile([P, UNIT_SLABS * K], BF16, name="w3_rows%d" % w)
             nc.sync.dma_start(
-                out=rows[:].rearrange("p (s k) -> p s k", s=UNIT_SLABS),
+                out=rows[:],
                 in_=W3[w * UNIT_SLABS * P : (w + 1) * UNIT_SLABS * P, :].rearrange(
-                    "(s p) k -> p s k", p=P
+                    "(p s) k -> p (s k)", s=UNIT_SLABS
                 ),
             )
             w3_rows.append(rows)
+        mask = keep.tile([P, NEIGHBOURS], BF16)
+        nc.sync.dma_start(out=mask[:], in_=attention_mask)
         m2_rows = []
         for i in range(UNITS):
             rows = keep.tile([P, UNIT_SLABS * K], BF16, name="m2_rows%d" % i)
@@ -76,7 +77,7 @@ def tile_decoderlayer_pb_kernel(
         shift_all = keep.tile([P, CHANNELS], BF16)
         nc.sync.dma_start(out=shift_all[:], in_=ln1_b.partition_broadcast(P))
 
-        zeros = keep.tile([P, CHANNELS], BF16)
+        zeros = keep.tile([P, HALF], BF16)
         nc.vector.memset(zeros[:], 0.0)
         identity = keep.tile([P, P], F32)
         make_identity(nc, identity[:])
@@ -86,8 +87,6 @@ def tile_decoderlayer_pb_kernel(
         nc.scalar.activation(
             out=table_warm[:], in_=eps[:], func=ACT.Abs_reciprocal_sqrt, bias=eps[:], scale=1.0
         )
-        mask = keep.tile([P, NEIGHBOURS], F32)
-        nc.vector.tensor_copy(out=mask[:], in_=mask_bf[:])
 
         def split_unit(rows, row_factors):
             split = split_pool.tile([P, UNIT_SLABS * K], BF16)
@@ -96,7 +95,8 @@ def tile_decoderlayer_pb_kernel(
                 source = rows[:, values].rearrange("p (g u e) -> p u g e", g=GROUPS, u=HALVES)
                 target = split[:, values].rearrange("p (u g e) -> p u g e", u=HALVES, g=GROUPS)
                 if row_factors is None:
-                    nc.vector.tensor_copy(out=target, in_=source)
+                    copy = nc.vector.tensor_copy if s == 0 else nc.scalar.copy
+                    copy(out=target, in_=source)
                 else:
                     nc.vector.tensor_scalar_mul(out=target, in0=source, scalar1=row_factors[s])
             return split
@@ -110,11 +110,15 @@ def tile_decoderlayer_pb_kernel(
                     nc.tensor.transpose(bank[:, s, u, :], words[:, block], identity[:])
             return bank
 
-        def regroup_unit(bank):
+        def regroup_unit(bank, order):
             grouped = grouped_pool.tile([P, UNIT_SLABS * P * PACK], BF16, align_bytes=64)
+            sizes = {"s": UNIT_SLABS, "r": P, "u": HALVES}
+            first, second, third = order.split()
             nc.scalar.copy(
-                out=grouped[:].bitcast(F32).rearrange("p (s r u) -> p s r u", s=UNIT_SLABS, u=HALVES),
-                in_=bank[:].rearrange("p s u r -> p s r u"),
+                out=grouped[:].bitcast(F32).rearrange(
+                    "p (a b c) -> p a b c", b=sizes[second], c=sizes[third]
+                ),
+                in_=bank[:].rearrange("p s u r -> p " + order),
             )
             return grouped
 
@@ -126,14 +130,16 @@ def tile_decoderlayer_pb_kernel(
 
         def keep_clock(matmuls):
             for j in range(matmuls):
-                nc.tensor.matmul(out=acc[:], lhsT=zeros[:, :P], rhs=zeros[:], start=True, stop=True)
+                nc.tensor.matmul(
+                    out=acc[:, :HALF], lhsT=zeros[:, :P], rhs=zeros[:], start=True, stop=True
+                )
 
         keep_clock(WARM_FIRST)
 
         w3_codes = keep.tile([P, CHANNELS], U32, align_bytes=64)
         w3_scales = keep.tile([P, CHANNELS], U8, align_bytes=64)
         w3_split = [split_unit(w3_rows[w], None) for w in range(W3_UNITS)]
-        w3_grouped = [regroup_unit(transpose_unit(w3_split[w])) for w in range(W3_UNITS)]
+        w3_grouped = [regroup_unit(transpose_unit(w3_split[w]), "r s u") for w in range(W3_UNITS)]
 
         def quantise_w3_unit(w):
             channels = slice(w * UNIT_SLABS * P, (w + 1) * UNIT_SLABS * P)
@@ -152,7 +158,7 @@ def tile_decoderlayer_pb_kernel(
             bank = transpose_unit(m2_split[i])
             codes = mx_pool.tile([P, UNIT_SLABS * P], U32, align_bytes=64)
             scales = mx_pool.tile([P, UNIT_SLABS * P], U8, align_bytes=64)
-            quantise_unit(regroup_unit(bank), codes[:], scales[:])
+            quantise_unit(regroup_unit(bank, "s r u"), codes[:], scales[:])
             m2_codes[i] = codes
             m2_scales[i] = scales
 
@@ -184,17 +190,18 @@ def tile_decoderlayer_pb_kernel(
         multiplied = 0
         for i in range(AHEAD):
             split_m2_unit(i)
-            if i < W3_UNITS:
-                quantise_w3_unit(i)
+        quantise_w3_unit(0)
         for first in range(0, UNITS, RUN):
             for i in range(first, first + RUN):
                 if i + AHEAD < UNITS:
                     split_m2_unit(i + AHEAD)
                     if i + AHEAD == UNITS - 1:
                         residual()
+                if i == 0:
+                    quantise_w3_unit(1)
                 prepare_unit(i)
                 if first == 0 and i + 1 < RUN:
-                    keep_clock(1)
+                    keep_clock(WARM_NEXT)
             ready = main_units if first + RUN == UNITS else first + RUN - LAG
             for i in range(multiplied, ready):
                 multiply_unit(i, acc, slice(0, CHANNELS), 0, main_units - 1)

@@ -23,11 +23,12 @@ GROUPS = K // 32
 UNIT_SLABS = 2
 UNITS = NEIGHBOURS // UNIT_SLABS
 W3_UNITS = CHANNELS // (P * UNIT_SLABS)
-RUN = 4
+RUNS = (4, 3, 3, 3, 3)
 AHEAD = 3
-LAG = 2
+LAG = 3
 TAIL = 3
 WARM_FIRST = 8
+WARM_UNITS = 3
 WARM_NEXT = 2
 SCALE = 30.0
 EPS = 1e-5
@@ -154,6 +155,12 @@ def tile_decoderlayer_pb_kernel(
             row_factors = [mask[:, first + s : first + s + 1] for s in range(UNIT_SLABS)]
             m2_split[i] = split_unit(m2_rows[i], row_factors)
 
+        def split_until(end):
+            for i in range(len(m2_split), min(end, UNITS)):
+                split_m2_unit(i)
+                if i == UNITS - 1:
+                    residual()
+
         def prepare_unit(i):
             bank = transpose_unit(m2_split[i])
             codes = mx_pool.tile([P, UNIT_SLABS * P], U32, align_bytes=64)
@@ -188,24 +195,23 @@ def tile_decoderlayer_pb_kernel(
 
         main_units = UNITS - TAIL
         multiplied = 0
-        for i in range(AHEAD):
-            split_m2_unit(i)
+        split_until(AHEAD)
         quantise_w3_unit(0)
-        for first in range(0, UNITS, RUN):
-            for i in range(first, first + RUN):
-                if i + AHEAD < UNITS:
-                    split_m2_unit(i + AHEAD)
-                    if i + AHEAD == UNITS - 1:
-                        residual()
+        first = 0
+        for run in RUNS:
+            last = first + run - 1
+            for i in range(first, last + 1):
+                split_until(i + AHEAD + 1)
                 if i == 0:
                     quantise_w3_unit(1)
                 prepare_unit(i)
-                if first == 0 and i + 1 < RUN:
+                if i < WARM_UNITS:
                     keep_clock(WARM_NEXT)
-            ready = main_units if first + RUN == UNITS else first + RUN - LAG
+            ready = main_units if last == UNITS - 1 else last + 1 - LAG
             for i in range(multiplied, ready):
                 multiply_unit(i, acc, slice(0, CHANNELS), 0, main_units - 1)
             multiplied = ready
+            first = last + 1
         halves = [slice(h * HALF, (h + 1) * HALF) for h in range(2)]
         for h in range(2):
             for i in range(main_units, UNITS):

@@ -27,7 +27,8 @@ RUNS = (4, 3, 3, 3, 3)
 AHEAD = 3
 LAG = 3
 TAIL = 3
-WARM_FIRST = 8
+TAIL_CHANNELS = ((0, 256, "acc_tail0"), (256, 384, "acc_tail1"), (384, 512, "acc"))
+WARM_FIRST = 11
 WARM_UNITS = 3
 WARM_NEXT = 2
 SCALE = 30.0
@@ -126,8 +127,7 @@ def tile_decoderlayer_pb_kernel(
         def quantise_unit(grouped, codes, scales):
             nc.vector.quantize_mx(out=codes.bitcast(FP8X4), scales=scales, in_=grouped[:])
 
-        acc = acc_pool.tile([P, CHANNELS], F32)
-        acc_tail = [acc_pool.tile([P, HALF], F32, name="acc_tail%d" % h) for h in range(2)]
+        acc = acc_pool.tile([P, CHANNELS], F32, name="acc")
 
         def keep_clock(matmuls):
             for j in range(matmuls):
@@ -140,7 +140,10 @@ def tile_decoderlayer_pb_kernel(
         w3_codes = keep.tile([P, CHANNELS], U32, align_bytes=64)
         w3_scales = keep.tile([P, CHANNELS], U8, align_bytes=64)
         w3_split = [split_unit(w3_rows[w], None) for w in range(W3_UNITS)]
-        w3_grouped = [regroup_unit(transpose_unit(w3_split[w]), "r s u") for w in range(W3_UNITS)]
+        w3_grouped = []
+        for w in range(W3_UNITS):
+            w3_grouped.append(regroup_unit(transpose_unit(w3_split[w]), "r s u"))
+            keep_clock(WARM_NEXT)
 
         def quantise_w3_unit(w):
             channels = slice(w * UNIT_SLABS * P, (w + 1) * UNIT_SLABS * P)
@@ -212,34 +215,43 @@ def tile_decoderlayer_pb_kernel(
                 multiply_unit(i, acc, slice(0, CHANNELS), 0, main_units - 1)
             multiplied = ready
             first = last + 1
-        halves = [slice(h * HALF, (h + 1) * HALF) for h in range(2)]
-        for h in range(2):
-            for i in range(main_units, UNITS):
-                multiply_unit(i, acc_tail[h], halves[h], main_units, UNITS - 1)
 
         x_main = keep.tile([P, CHANNELS], F32)
         nc.vector.scalar_tensor_tensor(
             out=x_main[:], in0=acc[:], scalar=1.0 / SCALE, in1=base[:], op0=ALU.mult, op1=ALU.add
         )
         x = keep.tile([P, CHANNELS], F32)
-        stats = keep.tile([P, 2, 6], F32)
-        for h in range(2):
+        stats = keep.tile([P, len(TAIL_CHANNELS), 6], F32)
+
+        def part_stats(j):
+            begin, end, bank = TAIL_CHANNELS[j]
+            nc.vector.bn_stats(out=stats[:, j, :], in_=x[:, begin:end])
+
+        for j, (begin, end, bank) in enumerate(TAIL_CHANNELS):
+            channels = slice(begin, end)
+            group = acc_pool.tile([P, end - begin], F32, name=bank)
+            for i in range(main_units, UNITS):
+                multiply_unit(i, group, channels, main_units, UNITS - 1)
             nc.vector.scalar_tensor_tensor(
-                out=x[:, halves[h]], in0=acc_tail[h][:], scalar=1.0 / SCALE, in1=x_main[:, halves[h]],
+                out=x[:, channels], in0=group[:], scalar=1.0 / SCALE, in1=x_main[:, channels],
                 op0=ALU.mult, op1=ALU.add,
             )
-            nc.vector.bn_stats(out=stats[:, h, :], in_=x[:, halves[h]])
+            if j > 0:
+                part_stats(j - 1)
+        part_stats(len(TAIL_CHANNELS) - 1)
         mean_var = keep.tile([P, 2], F32)
-        nc.vector.bn_aggr(out=mean_var[:], in_=stats[:].rearrange("p h s -> p (h s)"))
+        nc.vector.bn_aggr(out=mean_var[:], in_=stats[:].rearrange("p j s -> p (j s)"))
         inv_std = keep.tile([P, 1], F32)
         nc.scalar.activation(
             out=inv_std[:], in_=mean_var[:, 1:2], func=ACT.Abs_reciprocal_sqrt, bias=eps[:], scale=1.0
         )
+        halves = [slice(h * HALF, (h + 1) * HALF) for h in range(2)]
         centred = keep.tile([P, CHANNELS], F32)
-        nc.vector.scalar_tensor_tensor(
-            out=centred[:], in0=x[:], scalar=mean_var[:, 0:1], in1=gain_all[:],
-            op0=ALU.subtract, op1=ALU.mult,
-        )
+        for channels in halves:
+            nc.vector.scalar_tensor_tensor(
+                out=centred[:, channels], in0=x[:, channels], scalar=mean_var[:, 0:1],
+                in1=gain_all[:, channels], op0=ALU.subtract, op1=ALU.mult,
+            )
         result = keep.tile([P, CHANNELS], F32)
         for channels, queue in zip(halves, (nc.sync, nc.scalar)):
             nc.vector.scalar_tensor_tensor(

from contextlib import ExitStack

import concourse.mybir as mybir
from concourse.masks import make_identity

F32 = mybir.dt.float32
BF16 = mybir.dt.bfloat16
U32 = mybir.dt.uint32
U8 = mybir.dt.uint8
FP8X4 = mybir.dt.float8_e4m3fn_x4
ALU = mybir.AluOpType
ACT = mybir.ActivationFunctionType

P = 128
NEIGHBOURS = 32
K = 512
CHANNELS = 512
HALF = CHANNELS // 2
PACK = 4
WORDS = K // 2
HALVES = WORDS // P
GROUPS = K // 32
UNIT_SLABS = 2
UNITS = NEIGHBOURS // UNIT_SLABS
W3_UNITS = CHANNELS // (P * UNIT_SLABS)
RUNS = (4, 3, 3, 3, 3)
AHEAD = 3
LAG = 3
TAIL = 3
TAIL_CHANNELS = ((0, 256, "acc_tail0"), (256, 384, "acc_tail1"), (384, 512, "acc"))
WARM_FIRST = 11
WARM_UNITS = 3
WARM_NEXT = 2
SCALE = 30.0
EPS = 1e-5

FLOPS = 2 * P * NEIGHBOURS * K * CHANNELS


def tile_decoderlayer_pb_kernel(
    tc, m2, W3, b3, attention_mask, node_features, ln1_w, ln1_b, out
):
    nc = tc.nc
    with ExitStack() as ctx:
        ctx.enter_context(tc.manual_schedule())
        keep = ctx.enter_context(tc.tile_pool(name="keep", bufs=1))
        grouped_pool = ctx.enter_context(tc.tile_pool(name="grouped", bufs=4))
        split_pool = ctx.enter_context(tc.tile_pool(name="split", bufs=AHEAD + 4))
        mx_pool = ctx.enter_context(tc.tile_pool(name="mx", bufs=UNITS))
        bank_pool = ctx.enter_context(tc.psum_pool(name="banks", bufs=5))
        acc_pool = ctx.enter_context(tc.psum_pool(name="acc", bufs=1))

        w3_rows = []
        for w in range(W3_UNITS):
            rows = keep.tile([P, UNIT_SLABS * K], BF16, name="w3_rows%d" % w)
            nc.sync.dma_start(
                out=rows[:],
                in_=W3[w * UNIT_SLABS * P : (w + 1) * UNIT_SLABS * P, :].rearrange(
                    "(p s) k -> p (s k)", s=UNIT_SLABS
                ),
            )
            w3_rows.append(rows)
        mask = keep.tile([P, NEIGHBOURS], BF16)
        nc.sync.dma_start(out=mask[:], in_=attention_mask)
        m2_rows = []
        for i in range(UNITS):
            rows = keep.tile([P, UNIT_SLABS * K], BF16, name="m2_rows%d" % i)
            nc.sync.dma_start(
                out=rows[:].rearrange("p (s k) -> p s k", s=UNIT_SLABS),
                in_=m2[:, i * UNIT_SLABS : (i + 1) * UNIT_SLABS, :],
            )
            m2_rows.append(rows)
        nodes_bf = keep.tile([P, CHANNELS], BF16)
        nc.sync.dma_start(out=nodes_bf[:], in_=node_features)
        b3_all = keep.tile([P, CHANNELS], BF16)
        nc.sync.dma_start(out=b3_all[:], in_=b3.partition_broadcast(P))
        gain_all = keep.tile([P, CHANNELS], BF16)
        nc.sync.dma_start(out=gain_all[:], in_=ln1_w.partition_broadcast(P))
        shift_all = keep.tile([P, CHANNELS], BF16)
        nc.sync.dma_start(out=shift_all[:], in_=ln1_b.partition_broadcast(P))

        zeros = keep.tile([P, HALF], BF16)
        nc.vector.memset(zeros[:], 0.0)
        identity = keep.tile([P, P], F32)
        make_identity(nc, identity[:])
        eps = keep.tile([P, 1], F32)
        nc.vector.memset(eps[:], EPS)
        table_warm = keep.tile([P, 1], F32)
        nc.scalar.activation(
            out=table_warm[:], in_=eps[:], func=ACT.Abs_reciprocal_sqrt, bias=eps[:], scale=1.0
        )

        def split_unit(rows, row_factors):
            split = split_pool.tile([P, UNIT_SLABS * K], BF16)
            for s in range(UNIT_SLABS):
                values = slice(s * K, (s + 1) * K)
                source = rows[:, values].rearrange("p (g u e) -> p u g e", g=GROUPS, u=HALVES)
                target = split[:, values].rearrange("p (u g e) -> p u g e", u=HALVES, g=GROUPS)
                if row_factors is None:
                    copy = nc.vector.tensor_copy if s == 0 else nc.scalar.copy
                    copy(out=target, in_=source)
                else:
                    nc.vector.tensor_scalar_mul(out=target, in0=source, scalar1=row_factors[s])
            return split

        def transpose_unit(split):
            words = split[:].bitcast(F32)
            bank = bank_pool.tile([P, UNIT_SLABS, HALVES, P], F32)
            for s in range(UNIT_SLABS):
                for u in range(HALVES):
                    block = slice(s * WORDS + u * P, s * WORDS + (u + 1) * P)
                    nc.tensor.transpose(bank[:, s, u, :], words[:, block], identity[:])
            return bank

        def regroup_unit(bank, order):
            grouped = grouped_pool.tile([P, UNIT_SLABS * P * PACK], BF16, align_bytes=64)
            sizes = {"s": UNIT_SLABS, "r": P, "u": HALVES}
            first, second, third = order.split()
            nc.scalar.copy(
                out=grouped[:].bitcast(F32).rearrange(
                    "p (a b c) -> p a b c", b=sizes[second], c=sizes[third]
                ),
                in_=bank[:].rearrange("p s u r -> p " + order),
            )
            return grouped

        def quantise_unit(grouped, codes, scales):
            nc.vector.quantize_mx(out=codes.bitcast(FP8X4), scales=scales, in_=grouped[:])

        acc = acc_pool.tile([P, CHANNELS], F32, name="acc")

        def keep_clock(matmuls):
            for j in range(matmuls):
                nc.tensor.matmul(
                    out=acc[:, :HALF], lhsT=zeros[:, :P], rhs=zeros[:], start=True, stop=True
                )

        keep_clock(WARM_FIRST)

        w3_codes = keep.tile([P, CHANNELS], U32, align_bytes=64)
        w3_scales = keep.tile([P, CHANNELS], U8, align_bytes=64)
        w3_split = [split_unit(w3_rows[w], None) for w in range(W3_UNITS)]
        w3_grouped = []
        for w in range(W3_UNITS):
            w3_grouped.append(regroup_unit(transpose_unit(w3_split[w]), "r s u"))
            keep_clock(WARM_NEXT)

        def quantise_w3_unit(w):
            channels = slice(w * UNIT_SLABS * P, (w + 1) * UNIT_SLABS * P)
            quantise_unit(w3_grouped[w], w3_codes[:, channels], w3_scales[:, channels])

        m2_codes = {}
        m2_scales = {}
        m2_split = {}

        def split_m2_unit(i):
            first = i * UNIT_SLABS
            row_factors = [mask[:, first + s : first + s + 1] for s in range(UNIT_SLABS)]
            m2_split[i] = split_unit(m2_rows[i], row_factors)

        def split_until(end):
            for i in range(len(m2_split), min(end, UNITS)):
                split_m2_unit(i)
                if i == UNITS - 1:
                    residual()

        def prepare_unit(i):
            bank = transpose_unit(m2_split[i])
            codes = mx_pool.tile([P, UNIT_SLABS * P], U32, align_bytes=64)
            scales = mx_pool.tile([P, UNIT_SLABS * P], U8, align_bytes=64)
            quantise_unit(regroup_unit(bank, "s r u"), codes[:], scales[:])
            m2_codes[i] = codes
            m2_scales[i] = scales

        def multiply_unit(i, group, channels, first_unit, last_unit):
            for s in range(UNIT_SLABS):
                nodes = slice(s * P, (s + 1) * P)
                nc.tensor.matmul_mx(
                    out=group[:],
                    lhsT=m2_codes[i][:, nodes].bitcast(FP8X4),
                    lhsT_scale=m2_scales[i][:, nodes],
                    rhs=w3_codes[:, channels].bitcast(FP8X4),
                    rhs_scale=w3_scales[:, channels],
                    start=(i == first_unit and s == 0),
                    stop=(i == last_unit and s == UNIT_SLABS - 1),
                )

        base = keep.tile([P, CHANNELS], F32)

        def residual():
            kept = keep.tile([P, 1], F32)
            nc.vector.tensor_reduce(out=kept[:], in_=mask[:], axis=mybir.AxisListType.X, op=ALU.add)
            kept_scaled = keep.tile([P, 1], F32)
            nc.vector.tensor_scalar_mul(out=kept_scaled[:], in0=kept[:], scalar1=1.0 / SCALE)
            nc.vector.scalar_tensor_tensor(
                out=base[:], in0=b3_all[:], scalar=kept_scaled[:], in1=nodes_bf[:], op0=ALU.mult, op1=ALU.add
            )

        main_units = UNITS - TAIL
        multiplied = 0
        split_until(AHEAD)
        quantise_w3_unit(0)
        first = 0
        for run in RUNS:
            last = first + run - 1
            for i in range(first, last + 1):
                split_until(i + AHEAD + 1)
                if i == 0:
                    quantise_w3_unit(1)
                prepare_unit(i)
                if i < WARM_UNITS:
                    keep_clock(WARM_NEXT)
            ready = main_units if last == UNITS - 1 else last + 1 - LAG
            for i in range(multiplied, ready):
                multiply_unit(i, acc, slice(0, CHANNELS), 0, main_units - 1)
            multiplied = ready
            first = last + 1

        x_main = keep.tile([P, CHANNELS], F32)
        nc.vector.scalar_tensor_tensor(
            out=x_main[:], in0=acc[:], scalar=1.0 / SCALE, in1=base[:], op0=ALU.mult, op1=ALU.add
        )
        x = keep.tile([P, CHANNELS], F32)
        stats = keep.tile([P, len(TAIL_CHANNELS), 6], F32)

        def part_stats(j):
            begin, end, bank = TAIL_CHANNELS[j]
            nc.vector.bn_stats(out=stats[:, j, :], in_=x[:, begin:end])

        for j, (begin, end, bank) in enumerate(TAIL_CHANNELS):
            channels = slice(begin, end)
            group = acc_pool.tile([P, end - begin], F32, name=bank)
            for i in range(main_units, UNITS):
                multiply_unit(i, group, channels, main_units, UNITS - 1)
            nc.vector.scalar_tensor_tensor(
                out=x[:, channels], in0=group[:], scalar=1.0 / SCALE, in1=x_main[:, channels],
                op0=ALU.mult, op1=ALU.add,
            )
            if j > 0:
                part_stats(j - 1)
        part_stats(len(TAIL_CHANNELS) - 1)
        mean_var = keep.tile([P, 2], F32)
        nc.vector.bn_aggr(out=mean_var[:], in_=stats[:].rearrange("p j s -> p (j s)"))
        inv_std = keep.tile([P, 1], F32)
        nc.scalar.activation(
            out=inv_std[:], in_=mean_var[:, 1:2], func=ACT.Abs_reciprocal_sqrt, bias=eps[:], scale=1.0
        )
        halves = [slice(h * HALF, (h + 1) * HALF) for h in range(2)]
        centred = keep.tile([P, CHANNELS], F32)
        for channels in halves:
            nc.vector.scalar_tensor_tensor(
                out=centred[:, channels], in0=x[:, channels], scalar=mean_var[:, 0:1],
                in1=gain_all[:, channels], op0=ALU.subtract, op1=ALU.mult,
            )
        result = keep.tile([P, CHANNELS], F32)
        for channels, queue in zip(halves, (nc.sync, nc.scalar)):
            nc.vector.scalar_tensor_tensor(
                out=result[:, channels], in0=centred[:, channels], scalar=inv_std[:],
                in1=shift_all[:, channels], op0=ALU.mult, op1=ALU.add,
            )
            queue.dma_start(out=out[:, channels], in_=result[:, channels])
